import numpy as np
import ml_dtypes


def mxq(x, axis, fmt="e4m3"):
    dtype, down = {"e4m3": (ml_dtypes.float8_e4m3fn, 7), "e5m2": (ml_dtypes.float8_e5m2, 14)}[fmt]
    v = np.moveaxis(np.asarray(x, np.float32).astype(ml_dtypes.bfloat16).astype(np.float64), axis, -1)
    blocks = v.reshape(v.shape[:-1] + (-1, 32))
    amax = np.abs(blocks).max(-1, keepdims=True)
    byte = np.maximum(np.where(amax > 0, np.frexp(amax)[1] - 1 + 127, 0) - down, 1)
    scale = np.exp2(byte - 127.0)
    codes = (blocks / scale).astype(np.float32).astype(dtype).astype(np.float64)
    return np.moveaxis((codes * scale).reshape(v.shape), -1, axis)


WIDE = False


def mx_kscale(k):
    if not WIDE:
        return np.ones(k)
    levels = np.array([10, -10, 5, -5, 0])
    a = np.random.permutation(np.resize(levels, k // 512 * 4)).reshape(k // 512, 4)
    idx = np.arange(k)
    return np.exp2(a[idx // 512, idx % 128 // 32])


BF16 = ml_dtypes.bfloat16


def bf(x):
    return np.asarray(x, np.float32).astype(BF16)


def f64(x):
    return np.asarray(x).astype(np.float64)


B, IN, H = 4096, 512, 512


def sigmoid(v):
    return 1.0 / (1.0 + np.exp(-v))


def setup_inputs():
    s = mx_kscale(IN)
    return {'input': bf(np.random.standard_normal((B, IN)) * s),
            'state': bf(np.random.standard_normal((B, H))),
            'c': bf(np.tanh(np.random.standard_normal((B, H)))),
            'W2': bf(np.random.standard_normal((IN, H)) * 0.7 / np.sqrt(IN) / s[:, None]),
            'U2': bf(np.random.standard_normal((H, H)) * 0.7 / np.sqrt(H)),
            'bias_gate': bf(np.random.standard_normal((1, H)) * 0.5)}


def reference(input, state, c, W2, U2, bias_gate):
    h = f64(state)
    wComp2 = mxq(f64(input), 1, 'e4m3') @ mxq(f64(W2), 0, 'e4m3')
    uComp2 = mxq(h, 1, 'e4m3') @ mxq(f64(U2), 0, 'e4m3')
    z = sigmoid(wComp2 + uComp2 + f64(bias_gate))
    return z * h + (1.0 - z) * f64(c)

@@ -1,0 +1,208 @@
+from contextlib import ExitStack
+
+import concourse.mybir as mybir
+from concourse.masks import make_identity
+
+F32 = mybir.dt.float32
+BF16 = mybir.dt.bfloat16
+U32 = mybir.dt.uint32
+U8 = mybir.dt.uint8
+FP8X4 = mybir.dt.float8_e4m3fn_x4
+ALU = mybir.AluOpType
+ACT = mybir.ActivationFunctionType
+
+P = 128
+PACK = 4
+ROWS = 4096
+K = 512
+H = 512
+H_TILES = H // P
+
+CHUNK_TILES = 4
+CHUNK_ROWS = CHUNK_TILES * P
+N_CHUNKS = ROWS // CHUNK_ROWS
+UNIT_TILES = 2
+UNIT_ROWS = UNIT_TILES * P
+N_UNITS = ROWS // UNIT_ROWS
+UNITS_PER_CHUNK = CHUNK_TILES // UNIT_TILES
+
+FLOPS = 2 * 2 * ROWS * K * H
+
+
+def quantise_weight(nc, pool, copy, w, label):
+    raw = pool.tile([P, PACK, H], BF16, name=label + "_raw")
+    nc.sync.dma_start(
+        out=raw[:].rearrange("p (u e) h -> p u e h", u=2),
+        in_=w.rearrange("(u p e) h -> p u e h", u=2, e=2),
+    )
+    grouped = pool.tile([P, H, PACK], BF16, name=label + "_grouped", align_bytes=64)
+    for u in range(2):
+        cols = slice(u * 2 * P, (u + 1) * 2 * P)
+        copy(
+            out=grouped[:, cols, :].rearrange("p (e j) t -> p e j t", e=2),
+            in_=raw[:, :, cols].rearrange("p t (j e) -> p e j t", e=2),
+        )
+    codes = pool.tile([P, H], U32, name=label + "_codes", align_bytes=64)
+    scales = pool.tile([P, H], U8, name=label + "_scales", align_bytes=64)
+    nc.vector.quantize_mx(
+        out=codes[:].bitcast(FP8X4),
+        scales=scales[:],
+        in_=grouped[:].rearrange("p n t -> p (n t)"),
+    )
+    return codes, scales
+
+
+def tile_grulrcell_pb_t_kernel(tc, x, state, c, w2, u2, bias_gate, out):
+    nc = tc.nc
+    with ExitStack() as stack:
+        stack.enter_context(tc.manual_schedule())
+        const = stack.enter_context(tc.tile_pool(name="const", bufs=1))
+        resident = stack.enter_context(tc.tile_pool(name="resident", bufs=N_CHUNKS))
+        work = stack.enter_context(tc.tile_pool(name="work", bufs=3))
+        psum = stack.enter_context(tc.psum_pool(name="psum", bufs=2))
+
+        ident = const.tile([P, P], F32, name="ident")
+        make_identity(nc, ident[:])
+
+        bias_rows = const.tile([P, 2 * P], BF16, name="bias_rows")
+        nc.vector.memset(bias_rows[:], 0.0)
+        nc.scalar.dma_start(
+            out=bias_rows[0:2, :], in_=bias_gate.rearrange("o (u w) -> (o u) w", u=2)
+        )
+
+        w2_codes, w2_scales = quantise_weight(nc, const, nc.vector.tensor_copy, w2, "w2")
+        u2_codes, u2_scales = quantise_weight(nc, const, nc.scalar.copy, u2, "u2")
+
+        x_chunks, state_chunks, c_chunks = [], [], []
+        for ch in range(N_CHUNKS):
+            rows = slice(ch * CHUNK_ROWS, (ch + 1) * CHUNK_ROWS)
+            for src, chunks, label in (
+                (x, x_chunks, "x_chunk"),
+                (state, state_chunks, "state_chunk"),
+                (c, c_chunks, "c_chunk"),
+            ):
+                chunk = resident.tile([P, CHUNK_TILES, K], BF16, name=label)
+                nc.sync.dma_start(
+                    out=chunk[:], in_=src[rows, :].rearrange("(p t) k -> p t k", t=CHUNK_TILES)
+                )
+                chunks.append(chunk)
+
+        bias_ps = psum.tile([P, H], F32, name="bias_ps", tag="gate")
+        nc.tensor.transpose(bias_ps[:, 0:P], bias_rows[:].bitcast(F32), ident[:])
+        bias_col = const.tile([P, H_TILES], F32, name="bias_col")
+        nc.vector.tensor_copy(out=bias_col[:], in_=bias_ps[:, 0:2].bitcast(BF16))
+
+        def tiles_of(unit):
+            first = (unit % UNITS_PER_CHUNK) * UNIT_TILES
+            return unit // UNITS_PER_CHUNK, slice(first, first + UNIT_TILES)
+
+        def transpose_and_quantise(unit):
+            ch, tiles = tiles_of(unit)
+            grouped = work.tile([P, 2, UNIT_ROWS, PACK], BF16, name="grouped", align_bytes=64)
+            for operand, chunk in enumerate((x_chunks[ch], state_chunks[ch])):
+                words = chunk[:, tiles, :].bitcast(F32)
+                flipped = psum.tile([P, 2, UNIT_ROWS], F32, name="flipped", tag="flipped")
+                for tt in range(UNIT_TILES):
+                    for u in range(2):
+                        nc.tensor.transpose(
+                            flipped[:, u, tt * P : (tt + 1) * P],
+                            words[:, tt, u * P : (u + 1) * P],
+                            ident[:],
+                        )
+                nc.scalar.copy(
+                    out=grouped[:, operand, :, :].bitcast(F32),
+                    in_=flipped[:].rearrange("p u r -> p r u"),
+                )
+            codes = work.tile([P, 2 * UNIT_ROWS], U32, name="codes", align_bytes=64)
+            scales = work.tile([P, 2 * UNIT_ROWS], U8, name="scales", align_bytes=64)
+            nc.vector.quantize_mx(
+                out=codes[:].bitcast(FP8X4),
+                scales=scales[:],
+                in_=grouped[:].rearrange("p o r t -> p (o r t)"),
+            )
+            return codes, scales
+
+        def difference(unit):
+            ch, tiles = tiles_of(unit)
+            diff = work.tile([P, UNIT_TILES, H], F32, name="diff", bufs=4)
+            nc.vector.tensor_tensor(
+                out=diff[:],
+                in0=state_chunks[ch][:, tiles, :],
+                in1=c_chunks[ch][:, tiles, :],
+                op=ALU.subtract,
+            )
+            return diff
+
+        def gate(codes, scales):
+            x_cols = slice(0, UNIT_ROWS)
+            state_cols = slice(UNIT_ROWS, 2 * UNIT_ROWS)
+            gate_t = work.tile([P, H_TILES, UNIT_ROWS], F32, name="gate_t")
+            for pair in range(H_TILES // 2):
+                acc = psum.tile([P, 2, UNIT_ROWS], F32, name="acc", tag="acc")
+                for half in range(2):
+                    features = slice((2 * pair + half) * P, (2 * pair + half + 1) * P)
+                    nc.tensor.matmul_mx(
+                        out=acc[:, half, :],
+                        lhsT=w2_codes[:, features].bitcast(FP8X4),
+                        lhsT_scale=w2_scales[:, features],
+                        rhs=codes[:, x_cols].bitcast(FP8X4),
+                        rhs_scale=scales[:, x_cols],
+                        start=True,
+                        stop=False,
+                    )
+                    nc.tensor.matmul_mx(
+                        out=acc[:, half, :],
+                        lhsT=u2_codes[:, features].bitcast(FP8X4),
+                        lhsT_scale=u2_scales[:, features],
+                        rhs=codes[:, state_cols].bitcast(FP8X4),
+                        rhs_scale=scales[:, state_cols],
+                        start=False,
+                        stop=True,
+                    )
+                for half in range(2):
+                    m = 2 * pair + half
+                    nc.scalar.activation(
+                        out=gate_t[:, m, :],
+                        in_=acc[:, half, :],
+                        func=ACT.Sigmoid,
+                        bias=bias_col[:, m : m + 1],
+                        scale=1.0,
+                    )
+            return gate_t
+
+        def blend_and_store(unit, gate_t, diff):
+            ch, tiles = tiles_of(unit)
+            scaled = work.tile([P, UNIT_TILES, H], F32, name="scaled")
+            for tt in range(UNIT_TILES):
+                gate_rows = psum.tile([P, H], F32, name="gate_rows", tag="gate")
+                for m in range(H_TILES):
+                    nc.tensor.transpose(
+                        gate_rows[:, m * P : (m + 1) * P],
+                        gate_t[:, m, tt * P : (tt + 1) * P],
+                        ident[:],
+                    )
+                nc.vector.tensor_tensor(
+                    out=scaled[:, tt, :].rearrange("r (u j e) -> r u j e", u=2, e=2),
+                    in0=gate_rows[:].rearrange("r (u e j) -> r u j e", u=2, e=2),
+                    in1=diff[:, tt, :].rearrange("r (u j e) -> r u j e", u=2, e=2),
+                    op=ALU.mult,
+                )
+            result = work.tile([P, UNIT_TILES, H], F32, name="result", bufs=4)
+            nc.vector.tensor_tensor(
+                out=result[:], in0=scaled[:], in1=c_chunks[ch][:, tiles, :], op=ALU.add
+            )
+            rows = slice(ch * CHUNK_ROWS, (ch + 1) * CHUNK_ROWS)
+            nc.sync.dma_start(
+                out=out[rows, :].rearrange("(p t) h -> p t h", t=CHUNK_TILES)[:, tiles, :],
+                in_=result[:],
+            )
+
+        quantised, diffs, gates = {}, {}, {}
+        for step in range(N_UNITS + 2):
+            if step < N_UNITS:
+                quantised[step] = transpose_and_quantise(step)
+                diffs[step] = difference(step)
+            if 1 <= step <= N_UNITS:
+                gates[step - 1] = gate(*quantised[step - 1])
+            if step >= 2:
+                blend_and_store(step - 2, gates[step - 2], diffs[step - 2])

@@ -18,13 +18,9 @@ K = 512
 H = 512
 H_TILES = H // P
 
-CHUNK_TILES = 4
-CHUNK_ROWS = CHUNK_TILES * P
-N_CHUNKS = ROWS // CHUNK_ROWS
 UNIT_TILES = 2
 UNIT_ROWS = UNIT_TILES * P
 N_UNITS = ROWS // UNIT_ROWS
-UNITS_PER_CHUNK = CHUNK_TILES // UNIT_TILES
 
 FLOPS = 2 * 2 * ROWS * K * H
 
@@ -57,7 +53,7 @@ def tile_grulrcell_pb_t_kernel(tc, x, state, c, w2, u2, bias_gate, out):
     with ExitStack() as stack:
         stack.enter_context(tc.manual_schedule())
         const = stack.enter_context(tc.tile_pool(name="const", bufs=1))
-        resident = stack.enter_context(tc.tile_pool(name="resident", bufs=N_CHUNKS))
+        resident = stack.enter_context(tc.tile_pool(name="resident", bufs=N_UNITS))
         work = stack.enter_context(tc.tile_pool(name="work", bufs=3))
         psum = stack.enter_context(tc.psum_pool(name="psum", bufs=2))
 
@@ -73,46 +69,46 @@ def tile_grulrcell_pb_t_kernel(tc, x, state, c, w2, u2, bias_gate, out):
         w2_codes, w2_scales = quantise_weight(nc, const, nc.vector.tensor_copy, w2, "w2")
         u2_codes, u2_scales = quantise_weight(nc, const, nc.scalar.copy, u2, "u2")
 
-        x_chunks, state_chunks, c_chunks = [], [], []
-        for ch in range(N_CHUNKS):
-            rows = slice(ch * CHUNK_ROWS, (ch + 1) * CHUNK_ROWS)
-            for src, chunks, label in (
-                (x, x_chunks, "x_chunk"),
-                (state, state_chunks, "state_chunk"),
-                (c, c_chunks, "c_chunk"),
-            ):
-                chunk = resident.tile([P, CHUNK_TILES, K], BF16, name=label)
-                nc.sync.dma_start(
-                    out=chunk[:], in_=src[rows, :].rearrange("(p t) k -> p t k", t=CHUNK_TILES)
-                )
-                chunks.append(chunk)
+        def rows_of(dram, unit):
+            rows = slice(unit * UNIT_ROWS, (unit + 1) * UNIT_ROWS)
+            return dram[rows, :].rearrange("(p t) k -> p t k", t=UNIT_TILES)
 
-        bias_ps = psum.tile([P, H], F32, name="bias_ps", tag="gate")
+        x_units, state_units, c_units = [], [], []
+        for unit in range(N_UNITS):
+            for src, units, label in (
+                (x, x_units, "x_unit"),
+                (state, state_units, "state_unit"),
+                (c, c_units, "c_unit"),
+            ):
+                loaded = resident.tile([P, UNIT_TILES, K], BF16, name=label)
+                nc.sync.dma_start(out=loaded[:], in_=rows_of(src, unit))
+                units.append(loaded)
+
+        bias_ps = psum.tile([P, H], F32, name="bias_ps", tag="back")
         nc.tensor.transpose(bias_ps[:, 0:P], bias_rows[:].bitcast(F32), ident[:])
         bias_col = const.tile([P, H_TILES], F32, name="bias_col")
         nc.vector.tensor_copy(out=bias_col[:], in_=bias_ps[:, 0:2].bitcast(BF16))
 
-        def tiles_of(unit):
-            first = (unit % UNITS_PER_CHUNK) * UNIT_TILES
-            return unit // UNITS_PER_CHUNK, slice(first, first + UNIT_TILES)
+        def flip(loaded):
+            words = loaded[:].bitcast(F32)
+            flipped = psum.tile([P, 2, UNIT_ROWS], F32, name="flipped", tag="flipped", bufs=4)
+            for tt in range(UNIT_TILES):
+                for u in range(2):
+                    nc.tensor.transpose(
+                        flipped[:, u, tt * P : (tt + 1) * P],
+                        words[:, tt, u * P : (u + 1) * P],
+                        ident[:],
+                    )
+            return flipped
 
         def transpose_and_quantise(unit):
-            ch, tiles = tiles_of(unit)
             grouped = work.tile([P, 2, UNIT_ROWS, PACK], BF16, name="grouped", align_bytes=64)
-            for operand, chunk in enumerate((x_chunks[ch], state_chunks[ch])):
-                words = chunk[:, tiles, :].bitcast(F32)
-                flipped = psum.tile([P, 2, UNIT_ROWS], F32, name="flipped", tag="flipped")
-                for tt in range(UNIT_TILES):
-                    for u in range(2):
-                        nc.tensor.transpose(
-                            flipped[:, u, tt * P : (tt + 1) * P],
-                            words[:, tt, u * P : (u + 1) * P],
-                            ident[:],
-                        )
+            for operand, loaded in enumerate((x_units[unit], state_units[unit])):
                 nc.scalar.copy(
                     out=grouped[:, operand, :, :].bitcast(F32),
-                    in_=flipped[:].rearrange("p u r -> p r u"),
+                    in_=flip(loaded)[:].rearrange("p u r -> p r u"),
                 )
+            c_flipped = flip(c_units[unit])
             codes = work.tile([P, 2 * UNIT_ROWS], U32, name="codes", align_bytes=64)
             scales = work.tile([P, 2 * UNIT_ROWS], U8, name="scales", align_bytes=64)
             nc.vector.quantize_mx(
@@ -120,23 +116,20 @@ def tile_grulrcell_pb_t_kernel(tc, x, state, c, w2, u2, bias_gate, out):
                 scales=scales[:],
                 in_=grouped[:].rearrange("p o r t -> p (o r t)"),
             )
-            return codes, scales
-
-        def difference(unit):
-            ch, tiles = tiles_of(unit)
-            diff = work.tile([P, UNIT_TILES, H], F32, name="diff", bufs=4)
+            diff_t = work.tile([P, H_TILES, UNIT_ROWS], F32, name="diff_t")
             nc.vector.tensor_tensor(
-                out=diff[:],
-                in0=state_chunks[ch][:, tiles, :],
-                in1=c_chunks[ch][:, tiles, :],
+                out=diff_t[:].rearrange("p (u e) r -> p u e r", u=2),
+                in0=grouped[:, 1, :, :].rearrange("p r (u e) -> p u e r", u=2),
+                in1=c_flipped[:].bitcast(BF16).rearrange("p u (r e) -> p u e r", e=2),
                 op=ALU.subtract,
             )
-            return diff
+            return codes, scales, diff_t
 
-        def gate(codes, scales):
+        def gate_times_difference(codes, scales, diff_t):
             x_cols = slice(0, UNIT_ROWS)
             state_cols = slice(UNIT_ROWS, 2 * UNIT_ROWS)
             gate_t = work.tile([P, H_TILES, UNIT_ROWS], F32, name="gate_t")
+            scaled_t = work.tile([P, H_TILES, UNIT_ROWS], F32, name="scaled_t")
             for pair in range(H_TILES // 2):
                 acc = psum.tile([P, 2, UNIT_ROWS], F32, name="acc", tag="acc")
                 for half in range(2):
@@ -168,41 +161,38 @@ def tile_grulrcell_pb_t_kernel(tc, x, state, c, w2, u2, bias_gate, out):
                         bias=bias_col[:, m : m + 1],
                         scale=1.0,
                     )
-            return gate_t
+                both = slice(2 * pair, 2 * pair + 2)
+                nc.gpsimd.tensor_tensor(
+                    out=scaled_t[:, both, :],
+                    in0=gate_t[:, both, :],
+                    in1=diff_t[:, both, :],
+                    op=ALU.mult,
+                )
+            return scaled_t
 
-        def blend_and_store(unit, gate_t, diff):
-            ch, tiles = tiles_of(unit)
-            scaled = work.tile([P, UNIT_TILES, H], F32, name="scaled")
+        def add_c_and_store(unit, scaled_t):
+            result = work.tile([P, UNIT_TILES, H], F32, name="result", bufs=4)
             for tt in range(UNIT_TILES):
-                gate_rows = psum.tile([P, H], F32, name="gate_rows", tag="gate")
+                back = psum.tile([P, H], F32, name="back", tag="back")
                 for m in range(H_TILES):
                     nc.tensor.transpose(
-                        gate_rows[:, m * P : (m + 1) * P],
-                        gate_t[:, m, tt * P : (tt + 1) * P],
+                        back[:, m * P : (m + 1) * P],
+                        scaled_t[:, m, tt * P : (tt + 1) * P],
                         ident[:],
                     )
                 nc.vector.tensor_tensor(
-                    out=scaled[:, tt, :].rearrange("r (u j e) -> r u j e", u=2, e=2),
-                    in0=gate_rows[:].rearrange("r (u e j) -> r u j e", u=2, e=2),
-                    in1=diff[:, tt, :].rearrange("r (u j e) -> r u j e", u=2, e=2),
-                    op=ALU.mult,
+                    out=result[:, tt, :].rearrange("r (u j e) -> r u j e", u=2, e=2),
+                    in0=back[:].rearrange("r (u e j) -> r u j e", u=2, e=2),
+                    in1=c_units[unit][:, tt, :].rearrange("r (u j e) -> r u j e", u=2, e=2),
+                    op=ALU.add,
                 )
-            result = work.tile([P, UNIT_TILES, H], F32, name="result", bufs=4)
-            nc.vector.tensor_tensor(
-                out=result[:], in0=scaled[:], in1=c_chunks[ch][:, tiles, :], op=ALU.add
-            )
-            rows = slice(ch * CHUNK_ROWS, (ch + 1) * CHUNK_ROWS)
-            nc.sync.dma_start(
-                out=out[rows, :].rearrange("(p t) h -> p t h", t=CHUNK_TILES)[:, tiles, :],
-                in_=result[:],
-            )
+            nc.sync.dma_start(out=rows_of(out, unit), in_=result[:])
 
-        quantised, diffs, gates = {}, {}, {}
+        quantised, products = {}, {}
         for step in range(N_UNITS + 2):
             if step < N_UNITS:
                 quantised[step] = transpose_and_quantise(step)
-                diffs[step] = difference(step)
             if 1 <= step <= N_UNITS:
-                gates[step - 1] = gate(*quantised[step - 1])
+                products[step - 1] = gate_times_difference(*quantised[step - 1])
             if step >= 2:
-                blend_and_store(step - 2, gates[step - 2], diffs[step - 2])
+                add_c_and_store(step - 2, products[step - 2])

@@ -21,11 +21,13 @@ H_TILES = H // P
 UNIT_TILES = 2
 UNIT_ROWS = UNIT_TILES * P
 N_UNITS = ROWS // UNIT_ROWS
+GATE_LAG = 1
+BACK_LAG = 3
 
 FLOPS = 2 * 2 * ROWS * K * H
 
 
-def quantise_weight(nc, pool, copy, w, label):
+def quantise_weight(nc, pool, w, label):
     raw = pool.tile([P, PACK, H], BF16, name=label + "_raw")
     nc.sync.dma_start(
         out=raw[:].rearrange("p (u e) h -> p u e h", u=2),
@@ -34,7 +36,7 @@ def quantise_weight(nc, pool, copy, w, label):
     grouped = pool.tile([P, H, PACK], BF16, name=label + "_grouped", align_bytes=64)
     for u in range(2):
         cols = slice(u * 2 * P, (u + 1) * 2 * P)
-        copy(
+        nc.vector.tensor_copy(
             out=grouped[:, cols, :].rearrange("p (e j) t -> p e j t", e=2),
             in_=raw[:, :, cols].rearrange("p t (j e) -> p e j t", e=2),
         )
@@ -66,8 +68,8 @@ def tile_grulrcell_pb_t_kernel(tc, x, state, c, w2, u2, bias_gate, out):
             out=bias_rows[0:2, :], in_=bias_gate.rearrange("o (u w) -> (o u) w", u=2)
         )
 
-        w2_codes, w2_scales = quantise_weight(nc, const, nc.vector.tensor_copy, w2, "w2")
-        u2_codes, u2_scales = quantise_weight(nc, const, nc.scalar.copy, u2, "u2")
+        w2_codes, w2_scales = quantise_weight(nc, const, w2, "w2")
+        u2_codes, u2_scales = quantise_weight(nc, const, u2, "u2")
 
         def rows_of(dram, unit):
             rows = slice(unit * UNIT_ROWS, (unit + 1) * UNIT_ROWS)
@@ -129,7 +131,7 @@ def tile_grulrcell_pb_t_kernel(tc, x, state, c, w2, u2, bias_gate, out):
             x_cols = slice(0, UNIT_ROWS)
             state_cols = slice(UNIT_ROWS, 2 * UNIT_ROWS)
             gate_t = work.tile([P, H_TILES, UNIT_ROWS], F32, name="gate_t")
-            scaled_t = work.tile([P, H_TILES, UNIT_ROWS], F32, name="scaled_t")
+            scaled_t = work.tile([P, H_TILES, UNIT_ROWS], F32, name="scaled_t", bufs=4)
             for pair in range(H_TILES // 2):
                 acc = psum.tile([P, 2, UNIT_ROWS], F32, name="acc", tag="acc")
                 for half in range(2):
@@ -161,13 +163,7 @@ def tile_grulrcell_pb_t_kernel(tc, x, state, c, w2, u2, bias_gate, out):
                         bias=bias_col[:, m : m + 1],
                         scale=1.0,
                     )
-                both = slice(2 * pair, 2 * pair + 2)
-                nc.gpsimd.tensor_tensor(
-                    out=scaled_t[:, both, :],
-                    in0=gate_t[:, both, :],
-                    in1=diff_t[:, both, :],
-                    op=ALU.mult,
-                )
+            nc.gpsimd.tensor_tensor(out=scaled_t[:], in0=gate_t[:], in1=diff_t[:], op=ALU.mult)
             return scaled_t
 
         def add_c_and_store(unit, scaled_t):
@@ -186,13 +182,15 @@ def tile_grulrcell_pb_t_kernel(tc, x, state, c, w2, u2, bias_gate, out):
                     in1=c_units[unit][:, tt, :].rearrange("r (u j e) -> r u j e", u=2, e=2),
                     op=ALU.add,
                 )
-            nc.sync.dma_start(out=rows_of(out, unit), in_=result[:])
+                nc.sync.dma_start(out=rows_of(out, unit)[:, tt, :], in_=result[:, tt, :])
 
         quantised, products = {}, {}
-        for step in range(N_UNITS + 2):
+        for step in range(N_UNITS + BACK_LAG):
             if step < N_UNITS:
                 quantised[step] = transpose_and_quantise(step)
-            if 1 <= step <= N_UNITS:
-                products[step - 1] = gate_times_difference(*quantised[step - 1])
-            if step >= 2:
-                add_c_and_store(step - 2, products[step - 2])
+            if GATE_LAG <= step < N_UNITS + GATE_LAG:
+                unit = step - GATE_LAG
+                products[unit] = gate_times_difference(*quantised[unit])
+            if step >= BACK_LAG:
+                unit = step - BACK_LAG
+                add_c_and_store(unit, products[unit])

@@ -68,6 +68,9 @@ def tile_grulrcell_pb_t_kernel(tc, x, state, c, w2, u2, bias_gate, out):
             out=bias_rows[0:2, :], in_=bias_gate.rearrange("o (u w) -> (o u) w", u=2)
         )
 
+        warm = const.tile([P, 1], F32, name="warm")
+        nc.scalar.activation(out=warm[:], in_=ident[:, 0:1], func=ACT.Sigmoid)
+
         w2_codes, w2_scales = quantise_weight(nc, const, w2, "w2")
         u2_codes, u2_scales = quantise_weight(nc, const, u2, "u2")
 
@@ -118,7 +121,7 @@ def tile_grulrcell_pb_t_kernel(tc, x, state, c, w2, u2, bias_gate, out):
                 scales=scales[:],
                 in_=grouped[:].rearrange("p o r t -> p (o r t)"),
             )
-            diff_t = work.tile([P, H_TILES, UNIT_ROWS], F32, name="diff_t")
+            diff_t = work.tile([P, H_TILES, UNIT_ROWS], F32, name="diff_t", bufs=4)
             nc.vector.tensor_tensor(
                 out=diff_t[:].rearrange("p (u e) r -> p u e r", u=2),
                 in0=grouped[:, 1, :, :].rearrange("p r (u e) -> p u e r", u=2),
@@ -167,7 +170,7 @@ def tile_grulrcell_pb_t_kernel(tc, x, state, c, w2, u2, bias_gate, out):
             return scaled_t
 
         def add_c_and_store(unit, scaled_t):
-            result = work.tile([P, UNIT_TILES, H], F32, name="result", bufs=4)
+            result = work.tile([P, UNIT_TILES, H], F32, name="result", bufs=6)
             for tt in range(UNIT_TILES):
                 back = psum.tile([P, H], F32, name="back", tag="back")
                 for m in range(H_TILES):

@@ -17,37 +17,16 @@ ROWS = 4096
 K = 512
 H = 512
 H_TILES = H // P
+HALF = H // 2
 
 UNIT_TILES = 2
 UNIT_ROWS = UNIT_TILES * P
 N_UNITS = ROWS // UNIT_ROWS
+FLIP_LEAD = 1
 GATE_LAG = 1
-BACK_LAG = 3
+BACK_LAG = 2
 
 FLOPS = 2 * 2 * ROWS * K * H
-
-
-def quantise_weight(nc, pool, w, label):
-    raw = pool.tile([P, PACK, H], BF16, name=label + "_raw")
-    nc.sync.dma_start(
-        out=raw[:].rearrange("p (u e) h -> p u e h", u=2),
-        in_=w.rearrange("(u p e) h -> p u e h", u=2, e=2),
-    )
-    grouped = pool.tile([P, H, PACK], BF16, name=label + "_grouped", align_bytes=64)
-    for u in range(2):
-        cols = slice(u * 2 * P, (u + 1) * 2 * P)
-        nc.vector.tensor_copy(
-            out=grouped[:, cols, :].rearrange("p (e j) t -> p e j t", e=2),
-            in_=raw[:, :, cols].rearrange("p t (j e) -> p e j t", e=2),
-        )
-    codes = pool.tile([P, H], U32, name=label + "_codes", align_bytes=64)
-    scales = pool.tile([P, H], U8, name=label + "_scales", align_bytes=64)
-    nc.vector.quantize_mx(
-        out=codes[:].bitcast(FP8X4),
-        scales=scales[:],
-        in_=grouped[:].rearrange("p n t -> p (n t)"),
-    )
-    return codes, scales
 
 
 def tile_grulrcell_pb_t_kernel(tc, x, state, c, w2, u2, bias_gate, out):
@@ -59,40 +38,50 @@ def tile_grulrcell_pb_t_kernel(tc, x, state, c, w2, u2, bias_gate, out):
         work = stack.enter_context(tc.tile_pool(name="work", bufs=3))
         psum = stack.enter_context(tc.psum_pool(name="psum", bufs=2))
 
-        ident = const.tile([P, P], F32, name="ident")
-        make_identity(nc, ident[:])
-
-        bias_rows = const.tile([P, 2 * P], BF16, name="bias_rows")
-        nc.vector.memset(bias_rows[:], 0.0)
-        nc.scalar.dma_start(
-            out=bias_rows[0:2, :], in_=bias_gate.rearrange("o (u w) -> (o u) w", u=2)
-        )
-
-        warm = const.tile([P, 1], F32, name="warm")
-        nc.scalar.activation(out=warm[:], in_=ident[:, 0:1], func=ACT.Sigmoid)
-
-        w2_codes, w2_scales = quantise_weight(nc, const, w2, "w2")
-        u2_codes, u2_scales = quantise_weight(nc, const, u2, "u2")
-
         def rows_of(dram, unit):
             rows = slice(unit * UNIT_ROWS, (unit + 1) * UNIT_ROWS)
             return dram[rows, :].rearrange("(p t) k -> p t k", t=UNIT_TILES)
 
-        x_units, state_units, c_units = [], [], []
-        for unit in range(N_UNITS):
-            for src, units, label in (
-                (x, x_units, "x_unit"),
-                (state, state_units, "state_unit"),
-                (c, c_units, "c_unit"),
-            ):
-                loaded = resident.tile([P, UNIT_TILES, K], BF16, name=label)
-                nc.sync.dma_start(out=loaded[:], in_=rows_of(src, unit))
-                units.append(loaded)
+        x_units, state_units, c_units = {}, {}, {}
 
-        bias_ps = psum.tile([P, H], F32, name="bias_ps", tag="back")
-        nc.tensor.transpose(bias_ps[:, 0:P], bias_rows[:].bitcast(F32), ident[:])
-        bias_col = const.tile([P, H_TILES], F32, name="bias_col")
-        nc.vector.tensor_copy(out=bias_col[:], in_=bias_ps[:, 0:2].bitcast(BF16))
+        def load_unit(src, units, unit, label):
+            loaded = resident.tile([P, UNIT_TILES, K], BF16, name=label)
+            nc.sync.dma_start(out=loaded[:], in_=rows_of(src, unit))
+            units[unit] = loaded
+
+        def load_weight(w, label):
+            raw = const.tile([P, PACK, H], BF16, name=label)
+            nc.sync.dma_start(
+                out=raw[:].rearrange("p (u e) h -> p u e h", u=2),
+                in_=w.rearrange("(u p e) h -> p u e h", u=2, e=2),
+            )
+            return raw
+
+        load_unit(x, x_units, 0, "x_unit")
+        load_unit(state, state_units, 0, "state_unit")
+        w2_raw = load_weight(w2, "w2_raw")
+        u2_raw = load_weight(u2, "u2_raw")
+        load_unit(x, x_units, 1, "x_unit")
+        load_unit(state, state_units, 1, "state_unit")
+        for unit in range(2, N_UNITS + 2):
+            if unit < N_UNITS:
+                load_unit(x, x_units, unit, "x_unit")
+                load_unit(state, state_units, unit, "state_unit")
+            load_unit(c, c_units, unit - 2, "c_unit")
+
+        ident = const.tile([P, P], F32, name="ident")
+        make_identity(nc, ident[:])
+
+        bias_rows = const.tile([P, P], BF16, name="bias_rows")
+        nc.gpsimd.memset(bias_rows[:], 0.0)
+        nc.scalar.dma_start(
+            out=bias_rows[0:H_TILES, :], in_=bias_gate.rearrange("o (m p) -> (o m) p", m=H_TILES)
+        )
+        bias_words = const.tile([P, P], F32, name="bias_words")
+        nc.gpsimd.tensor_copy(out=bias_words[:], in_=bias_rows[:])
+
+        warm = const.tile([P, 1], F32, name="warm")
+        nc.scalar.activation(out=warm[:], in_=ident[:, 0:1], func=ACT.Sigmoid)
 
         def flip(loaded):
             words = loaded[:].bitcast(F32)
@@ -106,14 +95,16 @@ def tile_grulrcell_pb_t_kernel(tc, x, state, c, w2, u2, bias_gate, out):
                     )
             return flipped
 
-        def transpose_and_quantise(unit):
+        def transpose_operands(unit):
             grouped = work.tile([P, 2, UNIT_ROWS, PACK], BF16, name="grouped", align_bytes=64)
             for operand, loaded in enumerate((x_units[unit], state_units[unit])):
                 nc.scalar.copy(
                     out=grouped[:, operand, :, :].bitcast(F32),
                     in_=flip(loaded)[:].rearrange("p u r -> p r u"),
                 )
-            c_flipped = flip(c_units[unit])
+            return grouped
+
+        def quantise(grouped):
             codes = work.tile([P, 2 * UNIT_ROWS], U32, name="codes", align_bytes=64)
             scales = work.tile([P, 2 * UNIT_ROWS], U8, name="scales", align_bytes=64)
             nc.vector.quantize_mx(
@@ -121,20 +112,12 @@ def tile_grulrcell_pb_t_kernel(tc, x, state, c, w2, u2, bias_gate, out):
                 scales=scales[:],
                 in_=grouped[:].rearrange("p o r t -> p (o r t)"),
             )
-            diff_t = work.tile([P, H_TILES, UNIT_ROWS], F32, name="diff_t", bufs=4)
-            nc.vector.tensor_tensor(
-                out=diff_t[:].rearrange("p (u e) r -> p u e r", u=2),
-                in0=grouped[:, 1, :, :].rearrange("p r (u e) -> p u e r", u=2),
-                in1=c_flipped[:].bitcast(BF16).rearrange("p u (r e) -> p u e r", e=2),
-                op=ALU.subtract,
-            )
-            return codes, scales, diff_t
+            return codes, scales
 
-        def gate_times_difference(codes, scales, diff_t):
+        def gate(codes, scales):
             x_cols = slice(0, UNIT_ROWS)
             state_cols = slice(UNIT_ROWS, 2 * UNIT_ROWS)
             gate_t = work.tile([P, H_TILES, UNIT_ROWS], F32, name="gate_t")
-            scaled_t = work.tile([P, H_TILES, UNIT_ROWS], F32, name="scaled_t", bufs=4)
             for pair in range(H_TILES // 2):
                 acc = psum.tile([P, 2, UNIT_ROWS], F32, name="acc", tag="acc")
                 for half in range(2):
@@ -166,34 +149,89 @@ def tile_grulrcell_pb_t_kernel(tc, x, state, c, w2, u2, bias_gate, out):
                         bias=bias_col[:, m : m + 1],
                         scale=1.0,
                     )
-            nc.gpsimd.tensor_tensor(out=scaled_t[:], in0=gate_t[:], in1=diff_t[:], op=ALU.mult)
-            return scaled_t
+            return gate_t
 
-        def add_c_and_store(unit, scaled_t):
-            result = work.tile([P, UNIT_TILES, H], F32, name="result", bufs=6)
+        def blend_and_store(unit, gate_t):
+            state_part = work.tile([P, UNIT_TILES, H], F32, name="state_part", bufs=8)
+            c_part = work.tile([P, UNIT_TILES, H], F32, name="c_part")
             for tt in range(UNIT_TILES):
                 back = psum.tile([P, H], F32, name="back", tag="back")
                 for m in range(H_TILES):
                     nc.tensor.transpose(
                         back[:, m * P : (m + 1) * P],
-                        scaled_t[:, m, tt * P : (tt + 1) * P],
+                        gate_t[:, m, tt * P : (tt + 1) * P],
                         ident[:],
                     )
                 nc.vector.tensor_tensor(
-                    out=result[:, tt, :].rearrange("r (u j e) -> r u j e", u=2, e=2),
-                    in0=back[:].rearrange("r (u e j) -> r u j e", u=2, e=2),
-                    in1=c_units[unit][:, tt, :].rearrange("r (u j e) -> r u j e", u=2, e=2),
-                    op=ALU.add,
+                    out=state_part[:, tt, :],
+                    in0=back[:],
+                    in1=state_units[unit][:, tt, :],
+                    op=ALU.mult,
                 )
-                nc.sync.dma_start(out=rows_of(out, unit)[:, tt, :], in_=result[:, tt, :])
+                nc.vector.scalar_tensor_tensor(
+                    out=c_part[:, tt, :],
+                    in0=back[:],
+                    scalar=1.0,
+                    in1=c_units[unit][:, tt, :],
+                    op0=ALU.subtract,
+                    op1=ALU.mult,
+                )
+            if unit < N_UNITS - 1:
+                nc.gpsimd.tensor_tensor(
+                    out=state_part[:], in0=state_part[:], in1=c_part[:], op=ALU.subtract
+                )
+                nc.sync.dma_start(out=rows_of(out, unit), in_=state_part[:])
+            else:
+                for tt in range(UNIT_TILES):
+                    nc.vector.tensor_tensor(
+                        out=state_part[:, tt, :],
+                        in0=state_part[:, tt, :],
+                        in1=c_part[:, tt, :],
+                        op=ALU.subtract,
+                    )
+                    nc.sync.dma_start(out=rows_of(out, unit)[:, tt, :], in_=state_part[:, tt, :])
 
-        quantised, products = {}, {}
+        flipped_units = {0: transpose_operands(0)}
+        bias_ps = psum.tile([P, H], F32, name="bias_ps", tag="back")
+        nc.tensor.transpose(bias_ps[:, 0:P], bias_words[:], ident[:])
+        bias_col = const.tile([P, H_TILES], F32, name="bias_col")
+        nc.scalar.copy(out=bias_col[:], in_=bias_ps[:, 0:H_TILES])
+        quantised = {0: quantise(flipped_units[0])}
+
+        groups, operands = {}, {}
+        for label in ("w2", "u2"):
+            groups[label] = const.tile([P, H, PACK], BF16, name=label + "_grouped", align_bytes=64)
+            codes = const.tile([P, H], U32, name=label + "_codes", align_bytes=64)
+            scales = const.tile([P, H], U8, name=label + "_scales", align_bytes=64)
+            operands[label] = (codes, scales)
+        first, second = slice(0, HALF), slice(HALF, H)
+        for label, raw, cols, copy in (
+            ("w2", w2_raw, first, nc.vector.tensor_copy),
+            ("u2", u2_raw, first, nc.scalar.copy),
+            ("w2", w2_raw, second, nc.vector.tensor_copy),
+            ("u2", u2_raw, second, nc.vector.tensor_copy),
+        ):
+            copy(out=groups[label][:, cols, :], in_=raw[:, :, cols].rearrange("p t h -> p h t"))
+        for cols in (first, second):
+            for label in ("w2", "u2"):
+                codes, scales = operands[label]
+                nc.vector.quantize_mx(
+                    out=codes[:, cols].bitcast(FP8X4),
+                    scales=scales[:, cols],
+                    in_=groups[label][:, cols, :].rearrange("p h t -> p (h t)"),
+                )
+        w2_codes, w2_scales = operands["w2"]
+        u2_codes, u2_scales = operands["u2"]
+
+        gates = {}
         for step in range(N_UNITS + BACK_LAG):
-            if step < N_UNITS:
-                quantised[step] = transpose_and_quantise(step)
+            if step + FLIP_LEAD < N_UNITS:
+                flipped_units[step + FLIP_LEAD] = transpose_operands(step + FLIP_LEAD)
+            if 0 < step < N_UNITS:
+                quantised[step] = quantise(flipped_units[step])
             if GATE_LAG <= step < N_UNITS + GATE_LAG:
                 unit = step - GATE_LAG
-                products[unit] = gate_times_difference(*quantised[unit])
+                gates[unit] = gate(*quantised[unit])
             if step >= BACK_LAG:
                 unit = step - BACK_LAG
-                add_c_and_store(unit, products[unit])
+                blend_and_store(unit, gates[unit])

@@ -23,8 +23,8 @@ UNIT_TILES = 2
 UNIT_ROWS = UNIT_TILES * P
 N_UNITS = ROWS // UNIT_ROWS
 FLIP_LEAD = 1
-GATE_LAG = 1
-BACK_LAG = 2
+BACK_LAG = 1
+LAST_UNITS = 2
 
 FLOPS = 2 * 2 * ROWS * K * H
 
@@ -37,6 +37,20 @@ def tile_grulrcell_pb_t_kernel(tc, x, state, c, w2, u2, bias_gate, out):
         resident = stack.enter_context(tc.tile_pool(name="resident", bufs=N_UNITS))
         work = stack.enter_context(tc.tile_pool(name="work", bufs=3))
         psum = stack.enter_context(tc.psum_pool(name="psum", bufs=2))
+
+        ident = const.tile([P, P], F32, name="ident")
+        make_identity(nc, ident[:])
+
+        bias_rows = const.tile([H_TILES, P], BF16, name="bias_rows")
+        nc.sync.dma_start(
+            out=bias_rows[:], in_=bias_gate.rearrange("o (m p) -> (o m) p", m=H_TILES)
+        )
+        bias_words = const.tile([P, P], F32, name="bias_words")
+        nc.gpsimd.memset(bias_words[:], 0.0)
+        nc.gpsimd.tensor_copy(out=bias_words[0:H_TILES, :], in_=bias_rows[:])
+
+        warm = const.tile([P, 1], F32, name="warm")
+        nc.scalar.activation(out=warm[:], in_=ident[:, 0:1], func=ACT.Sigmoid)
 
         def rows_of(dram, unit):
             rows = slice(unit * UNIT_ROWS, (unit + 1) * UNIT_ROWS)
@@ -68,20 +82,6 @@ def tile_grulrcell_pb_t_kernel(tc, x, state, c, w2, u2, bias_gate, out):
                 load_unit(x, x_units, unit, "x_unit")
                 load_unit(state, state_units, unit, "state_unit")
             load_unit(c, c_units, unit - 2, "c_unit")
-
-        ident = const.tile([P, P], F32, name="ident")
-        make_identity(nc, ident[:])
-
-        bias_rows = const.tile([P, P], BF16, name="bias_rows")
-        nc.gpsimd.memset(bias_rows[:], 0.0)
-        nc.scalar.dma_start(
-            out=bias_rows[0:H_TILES, :], in_=bias_gate.rearrange("o (m p) -> (o m) p", m=H_TILES)
-        )
-        bias_words = const.tile([P, P], F32, name="bias_words")
-        nc.gpsimd.tensor_copy(out=bias_words[:], in_=bias_rows[:])
-
-        warm = const.tile([P, 1], F32, name="warm")
-        nc.scalar.activation(out=warm[:], in_=ident[:, 0:1], func=ACT.Sigmoid)
 
         def flip(loaded):
             words = loaded[:].bitcast(F32)
@@ -176,20 +176,21 @@ def tile_grulrcell_pb_t_kernel(tc, x, state, c, w2, u2, bias_gate, out):
                     op0=ALU.subtract,
                     op1=ALU.mult,
                 )
-            if unit < N_UNITS - 1:
-                nc.gpsimd.tensor_tensor(
-                    out=state_part[:], in0=state_part[:], in1=c_part[:], op=ALU.subtract
-                )
-                nc.sync.dma_start(out=rows_of(out, unit), in_=state_part[:])
-            else:
-                for tt in range(UNIT_TILES):
-                    nc.vector.tensor_tensor(
+                if unit >= N_UNITS - LAST_UNITS:
+                    last = unit == N_UNITS - 1 and tt == UNIT_TILES - 1
+                    subtract = nc.vector.tensor_tensor if last else nc.gpsimd.tensor_tensor
+                    subtract(
                         out=state_part[:, tt, :],
                         in0=state_part[:, tt, :],
                         in1=c_part[:, tt, :],
                         op=ALU.subtract,
                     )
                     nc.sync.dma_start(out=rows_of(out, unit)[:, tt, :], in_=state_part[:, tt, :])
+            if unit < N_UNITS - LAST_UNITS:
+                nc.gpsimd.tensor_tensor(
+                    out=state_part[:], in0=state_part[:], in1=c_part[:], op=ALU.subtract
+                )
+                nc.sync.dma_start(out=rows_of(out, unit), in_=state_part[:])
 
         flipped_units = {0: transpose_operands(0)}
         bias_ps = psum.tile([P, H], F32, name="bias_ps", tag="back")
@@ -229,9 +230,7 @@ def tile_grulrcell_pb_t_kernel(tc, x, state, c, w2, u2, bias_gate, out):
                 flipped_units[step + FLIP_LEAD] = transpose_operands(step + FLIP_LEAD)
             if 0 < step < N_UNITS:
                 quantised[step] = quantise(flipped_units[step])
-            if GATE_LAG <= step < N_UNITS + GATE_LAG:
-                unit = step - GATE_LAG
-                gates[unit] = gate(*quantised[unit])
             if step >= BACK_LAG:
-                unit = step - BACK_LAG
-                blend_and_store(unit, gates[unit])
+                blend_and_store(step - BACK_LAG, gates[step - BACK_LAG])
+            if step < N_UNITS:
+                gates[step] = gate(*quantised[step])

@@ -23,7 +23,7 @@ UNIT_TILES = 2
 UNIT_ROWS = UNIT_TILES * P
 N_UNITS = ROWS // UNIT_ROWS
 FLIP_LEAD = 1
-BACK_LAG = 1
+BACK_LAG = 2
 LAST_UNITS = 2
 
 FLOPS = 2 * 2 * ROWS * K * H
@@ -117,7 +117,7 @@ def tile_grulrcell_pb_t_kernel(tc, x, state, c, w2, u2, bias_gate, out):
         def gate(codes, scales):
             x_cols = slice(0, UNIT_ROWS)
             state_cols = slice(UNIT_ROWS, 2 * UNIT_ROWS)
-            gate_t = work.tile([P, H_TILES, UNIT_ROWS], F32, name="gate_t")
+            gate_t = work.tile([P, H_TILES, UNIT_ROWS], F32, name="gate_t", bufs=4)
             for pair in range(H_TILES // 2):
                 acc = psum.tile([P, 2, UNIT_ROWS], F32, name="acc", tag="acc")
                 for half in range(2):

@@ -177,7 +177,7 @@ def tile_grulrcell_pb_t_kernel(tc, x, state, c, w2, u2, bias_gate, out):
                     op1=ALU.mult,
                 )
                 if unit >= N_UNITS - LAST_UNITS:
-                    last = unit == N_UNITS - 1 and tt == UNIT_TILES - 1
+                    last = unit == N_UNITS - 1
                     subtract = nc.vector.tensor_tensor if last else nc.gpsimd.tensor_tensor
                     subtract(
                         out=state_part[:, tt, :],
@@ -226,11 +226,11 @@ def tile_grulrcell_pb_t_kernel(tc, x, state, c, w2, u2, bias_gate, out):
 
         gates = {}
         for step in range(N_UNITS + BACK_LAG):
-            if step + FLIP_LEAD < N_UNITS:
-                flipped_units[step + FLIP_LEAD] = transpose_operands(step + FLIP_LEAD)
             if 0 < step < N_UNITS:
                 quantised[step] = quantise(flipped_units[step])
             if step >= BACK_LAG:
                 blend_and_store(step - BACK_LAG, gates[step - BACK_LAG])
+            if step + FLIP_LEAD < N_UNITS:
+                flipped_units[step + FLIP_LEAD] = transpose_operands(step + FLIP_LEAD)
             if step < N_UNITS:
                 gates[step] = gate(*quantised[step])

@@ -85,7 +85,7 @@ def tile_grulrcell_pb_t_kernel(tc, x, state, c, w2, u2, bias_gate, out):
 
         def flip(loaded):
             words = loaded[:].bitcast(F32)
-            flipped = psum.tile([P, 2, UNIT_ROWS], F32, name="flipped", tag="flipped", bufs=4)
+            flipped = psum.tile([P, 2, UNIT_ROWS], F32, name="flipped", tag="flipped", bufs=3)
             for tt in range(UNIT_TILES):
                 for u in range(2):
                     nc.tensor.transpose(
@@ -155,7 +155,7 @@ def tile_grulrcell_pb_t_kernel(tc, x, state, c, w2, u2, bias_gate, out):
             state_part = work.tile([P, UNIT_TILES, H], F32, name="state_part", bufs=8)
             c_part = work.tile([P, UNIT_TILES, H], F32, name="c_part")
             for tt in range(UNIT_TILES):
-                back = psum.tile([P, H], F32, name="back", tag="back")
+                back = psum.tile([P, H], F32, name="back", tag="back", bufs=3)
                 for m in range(H_TILES):
                     nc.tensor.transpose(
                         back[:, m * P : (m + 1) * P],
@@ -193,7 +193,7 @@ def tile_grulrcell_pb_t_kernel(tc, x, state, c, w2, u2, bias_gate, out):
                 nc.sync.dma_start(out=rows_of(out, unit), in_=state_part[:])
 
         flipped_units = {0: transpose_operands(0)}
-        bias_ps = psum.tile([P, H], F32, name="bias_ps", tag="back")
+        bias_ps = psum.tile([P, H], F32, name="bias_ps", tag="back", bufs=3)
         nc.tensor.transpose(bias_ps[:, 0:P], bias_words[:], ident[:])
         bias_col = const.tile([P, H_TILES], F32, name="bias_col")
         nc.scalar.copy(out=bias_col[:], in_=bias_ps[:, 0:H_TILES])

@@ -40,6 +40,12 @@ def tile_grulrcell_pb_t_kernel(tc, x, state, c, w2, u2, bias_gate, out):
 
         ident = const.tile([P, P], F32, name="ident")
         make_identity(nc, ident[:])
+        plus = const.tile([P, P], BF16, name="plus")
+        make_identity(nc, plus[:])
+        minus = const.tile([P, P], BF16, name="minus")
+        nc.vector.tensor_scalar(
+            out=minus[:], in0=plus[:], scalar1=-1.0, scalar2=None, op0=ALU.mult
+        )
 
         bias_rows = const.tile([H_TILES, P], BF16, name="bias_rows")
         nc.sync.dma_start(
@@ -85,7 +91,7 @@ def tile_grulrcell_pb_t_kernel(tc, x, state, c, w2, u2, bias_gate, out):
 
         def flip(loaded):
             words = loaded[:].bitcast(F32)
-            flipped = psum.tile([P, 2, UNIT_ROWS], F32, name="flipped", tag="flipped", bufs=3)
+            flipped = psum.tile([P, 2, UNIT_ROWS], F32, name="flipped", tag="flipped", bufs=2)
             for tt in range(UNIT_TILES):
                 for u in range(2):
                     nc.tensor.transpose(
@@ -151,46 +157,73 @@ def tile_grulrcell_pb_t_kernel(tc, x, state, c, w2, u2, bias_gate, out):
                     )
             return gate_t
 
-        def blend_and_store(unit, gate_t):
-            state_part = work.tile([P, UNIT_TILES, H], F32, name="state_part", bufs=8)
+        def corner_difference(unit):
+            diff_t = psum.tile([P, P], F32, name="diff_t", tag="diff", bufs=1)
+            for loaded, sign, first in ((state_units[unit], plus, True), (c_units[unit], minus, False)):
+                nc.tensor.matmul(
+                    diff_t[:], lhsT=loaded[:, 0, 0:P], rhs=sign[:], start=first, stop=not first
+                )
+            return diff_t
+
+        def corner_product(gate_t, diff_t):
+            product_t = work.tile([P, P], F32, name="product_t")
+            nc.vector.tensor_tensor(
+                out=product_t[:], in0=gate_t[:, 0, 0:P], in1=diff_t[:], op=ALU.mult
+            )
+            return product_t
+
+        def subtract_and_store(unit, result, c_part, tiles, engine):
+            cols = slice(max(tiles.start * H, P), tiles.stop * H)
+            flat = result[:].rearrange("p t h -> p (t h)")
+            engine.tensor_tensor(
+                out=flat[:, cols],
+                in0=flat[:, cols],
+                in1=c_part[:].rearrange("p t h -> p (t h)")[:, cols],
+                op=ALU.subtract,
+            )
+            nc.sync.dma_start(out=rows_of(out, unit)[:, tiles, :], in_=result[:, tiles, :])
+
+        def blend_and_store(unit, gate_t, product_t, between):
+            result = work.tile([P, UNIT_TILES, H], F32, name="result", bufs=8)
             c_part = work.tile([P, UNIT_TILES, H], F32, name="c_part")
             for tt in range(UNIT_TILES):
                 back = psum.tile([P, H], F32, name="back", tag="back", bufs=3)
                 for m in range(H_TILES):
+                    corner = tt == 0 and m == 0
                     nc.tensor.transpose(
                         back[:, m * P : (m + 1) * P],
-                        gate_t[:, m, tt * P : (tt + 1) * P],
+                        product_t[:] if corner else gate_t[:, m, tt * P : (tt + 1) * P],
                         ident[:],
                     )
+                cols = slice(P if tt == 0 else 0, H)
                 nc.vector.tensor_tensor(
-                    out=state_part[:, tt, :],
-                    in0=back[:],
-                    in1=state_units[unit][:, tt, :],
+                    out=result[:, tt, cols],
+                    in0=back[:, cols],
+                    in1=state_units[unit][:, tt, cols],
                     op=ALU.mult,
                 )
+                if tt == 0:
+                    nc.vector.tensor_tensor(
+                        out=result[:, 0, 0:P],
+                        in0=back[:, 0:P],
+                        in1=c_units[unit][:, 0, 0:P],
+                        op=ALU.add,
+                    )
+                if tt == UNIT_TILES - 1:
+                    between()
                 nc.vector.scalar_tensor_tensor(
-                    out=c_part[:, tt, :],
-                    in0=back[:],
+                    out=c_part[:, tt, cols],
+                    in0=back[:, cols],
                     scalar=1.0,
-                    in1=c_units[unit][:, tt, :],
+                    in1=c_units[unit][:, tt, cols],
                     op0=ALU.subtract,
                     op1=ALU.mult,
                 )
                 if unit >= N_UNITS - LAST_UNITS:
-                    last = unit == N_UNITS - 1
-                    subtract = nc.vector.tensor_tensor if last else nc.gpsimd.tensor_tensor
-                    subtract(
-                        out=state_part[:, tt, :],
-                        in0=state_part[:, tt, :],
-                        in1=c_part[:, tt, :],
-                        op=ALU.subtract,
-                    )
-                    nc.sync.dma_start(out=rows_of(out, unit)[:, tt, :], in_=state_part[:, tt, :])
+                    engine = nc.vector if unit == N_UNITS - 1 else nc.gpsimd
+                    subtract_and_store(unit, result, c_part, slice(tt, tt + 1), engine)
             if unit < N_UNITS - LAST_UNITS:
-                nc.gpsimd.tensor_tensor(
-                    out=state_part[:], in0=state_part[:], in1=c_part[:], op=ALU.subtract
-                )
-                nc.sync.dma_start(out=rows_of(out, unit), in_=state_part[:])
+                subtract_and_store(unit, result, c_part, slice(0, UNIT_TILES), nc.gpsimd)
 
         flipped_units = {0: transpose_operands(0)}
         bias_ps = psum.tile([P, H], F32, name="bias_ps", tag="back", bufs=3)
@@ -224,12 +257,25 @@ def tile_grulrcell_pb_t_kernel(tc, x, state, c, w2, u2, bias_gate, out):
         w2_codes, w2_scales = operands["w2"]
         u2_codes, u2_scales = operands["u2"]
 
-        gates = {}
+        gates, products = {}, {}
         for step in range(N_UNITS + BACK_LAG):
             if 0 < step < N_UNITS:
                 quantised[step] = quantise(flipped_units[step])
+
+            corner_unit = step - 1
+            has_corner = 0 <= corner_unit < N_UNITS
+            if has_corner:
+                diff_t = corner_difference(corner_unit)
+
+            def corner_step():
+                if has_corner:
+                    products[corner_unit] = corner_product(gates[corner_unit], diff_t)
+
             if step >= BACK_LAG:
-                blend_and_store(step - BACK_LAG, gates[step - BACK_LAG])
+                unit = step - BACK_LAG
+                blend_and_store(unit, gates[unit], products[unit], corner_step)
+            else:
+                corner_step()
             if step + FLIP_LEAD < N_UNITS:
                 flipped_units[step + FLIP_LEAD] = transpose_operands(step + FLIP_LEAD)
             if step < N_UNITS:

@@ -173,7 +173,7 @@ def tile_grulrcell_pb_t_kernel(tc, x, state, c, w2, u2, bias_gate, out):
             return product_t
 
         def subtract_and_store(unit, result, c_part, tiles, engine):
-            cols = slice(max(tiles.start * H, P), tiles.stop * H)
+            cols = slice(tiles.start * H + (P if unit in products else 0), tiles.stop * H)
             flat = result[:].rearrange("p t h -> p (t h)")
             engine.tensor_tensor(
                 out=flat[:, cols],
@@ -183,26 +183,28 @@ def tile_grulrcell_pb_t_kernel(tc, x, state, c, w2, u2, bias_gate, out):
             )
             nc.sync.dma_start(out=rows_of(out, unit)[:, tiles, :], in_=result[:, tiles, :])
 
-        def blend_and_store(unit, gate_t, product_t, between):
-            result = work.tile([P, UNIT_TILES, H], F32, name="result", bufs=8)
+        def blend_and_store(unit, between):
+            gate_t = gates[unit]
+            result = work.tile([P, UNIT_TILES, H], F32, name="result", bufs=12)
             c_part = work.tile([P, UNIT_TILES, H], F32, name="c_part")
             for tt in range(UNIT_TILES):
                 back = psum.tile([P, H], F32, name="back", tag="back", bufs=3)
                 for m in range(H_TILES):
-                    corner = tt == 0 and m == 0
+                    corner = tt == 0 and m == 0 and unit in products
                     nc.tensor.transpose(
                         back[:, m * P : (m + 1) * P],
-                        product_t[:] if corner else gate_t[:, m, tt * P : (tt + 1) * P],
+                        products[unit][:] if corner else gate_t[:, m, tt * P : (tt + 1) * P],
                         ident[:],
                     )
-                cols = slice(P if tt == 0 else 0, H)
+                corner = tt == 0 and unit in products
+                cols = slice(P if corner else 0, H)
                 nc.vector.tensor_tensor(
                     out=result[:, tt, cols],
                     in0=back[:, cols],
                     in1=state_units[unit][:, tt, cols],
                     op=ALU.mult,
                 )
-                if tt == 0:
+                if corner:
                     nc.vector.tensor_tensor(
                         out=result[:, 0, 0:P],
                         in0=back[:, 0:P],
@@ -224,6 +226,8 @@ def tile_grulrcell_pb_t_kernel(tc, x, state, c, w2, u2, bias_gate, out):
                     subtract_and_store(unit, result, c_part, slice(tt, tt + 1), engine)
             if unit < N_UNITS - LAST_UNITS:
                 subtract_and_store(unit, result, c_part, slice(0, UNIT_TILES), nc.gpsimd)
+
+        gates, products = {}, {}
 
         flipped_units = {0: transpose_operands(0)}
         bias_ps = psum.tile([P, H], F32, name="bias_ps", tag="back", bufs=3)
@@ -257,13 +261,12 @@ def tile_grulrcell_pb_t_kernel(tc, x, state, c, w2, u2, bias_gate, out):
         w2_codes, w2_scales = operands["w2"]
         u2_codes, u2_scales = operands["u2"]
 
-        gates, products = {}, {}
         for step in range(N_UNITS + BACK_LAG):
             if 0 < step < N_UNITS:
                 quantised[step] = quantise(flipped_units[step])
 
             corner_unit = step - 1
-            has_corner = 0 <= corner_unit < N_UNITS
+            has_corner = 0 <= corner_unit < N_UNITS - LAST_UNITS
             if has_corner:
                 diff_t = corner_difference(corner_unit)
 
@@ -272,8 +275,7 @@ def tile_grulrcell_pb_t_kernel(tc, x, state, c, w2, u2, bias_gate, out):
                     products[corner_unit] = corner_product(gates[corner_unit], diff_t)
 
             if step >= BACK_LAG:
-                unit = step - BACK_LAG
-                blend_and_store(unit, gates[unit], products[unit], corner_step)
+                blend_and_store(step - BACK_LAG, corner_step)
             else:
                 corner_step()
             if step + FLIP_LEAD < N_UNITS:

from contextlib import ExitStack

import concourse.mybir as mybir
from concourse.masks import make_identity

F32 = mybir.dt.float32
BF16 = mybir.dt.bfloat16
U32 = mybir.dt.uint32
U8 = mybir.dt.uint8
FP8X4 = mybir.dt.float8_e4m3fn_x4
ALU = mybir.AluOpType
ACT = mybir.ActivationFunctionType

P = 128
PACK = 4
ROWS = 4096
K = 512
H = 512
H_TILES = H // P
HALF = H // 2

UNIT_TILES = 2
UNIT_ROWS = UNIT_TILES * P
N_UNITS = ROWS // UNIT_ROWS
FLIP_LEAD = 1
BACK_LAG = 2
LAST_UNITS = 2

FLOPS = 2 * 2 * ROWS * K * H


def tile_grulrcell_pb_t_kernel(tc, x, state, c, w2, u2, bias_gate, out):
    nc = tc.nc
    with ExitStack() as stack:
        stack.enter_context(tc.manual_schedule())
        const = stack.enter_context(tc.tile_pool(name="const", bufs=1))
        resident = stack.enter_context(tc.tile_pool(name="resident", bufs=N_UNITS))
        work = stack.enter_context(tc.tile_pool(name="work", bufs=3))
        psum = stack.enter_context(tc.psum_pool(name="psum", bufs=2))

        ident = const.tile([P, P], F32, name="ident")
        make_identity(nc, ident[:])
        plus = const.tile([P, P], BF16, name="plus")
        make_identity(nc, plus[:])
        minus = const.tile([P, P], BF16, name="minus")
        nc.vector.tensor_scalar(
            out=minus[:], in0=plus[:], scalar1=-1.0, scalar2=None, op0=ALU.mult
        )

        bias_rows = const.tile([H_TILES, P], BF16, name="bias_rows")
        nc.sync.dma_start(
            out=bias_rows[:], in_=bias_gate.rearrange("o (m p) -> (o m) p", m=H_TILES)
        )
        bias_words = const.tile([P, P], F32, name="bias_words")
        nc.gpsimd.memset(bias_words[:], 0.0)
        nc.gpsimd.tensor_copy(out=bias_words[0:H_TILES, :], in_=bias_rows[:])

        warm = const.tile([P, 1], F32, name="warm")
        nc.scalar.activation(out=warm[:], in_=ident[:, 0:1], func=ACT.Sigmoid)

        def rows_of(dram, unit):
            rows = slice(unit * UNIT_ROWS, (unit + 1) * UNIT_ROWS)
            return dram[rows, :].rearrange("(p t) k -> p t k", t=UNIT_TILES)

        x_units, state_units, c_units = {}, {}, {}

        def load_unit(src, units, unit, label):
            loaded = resident.tile([P, UNIT_TILES, K], BF16, name=label)
            nc.sync.dma_start(out=loaded[:], in_=rows_of(src, unit))
            units[unit] = loaded

        def load_weight(w, label):
            raw = const.tile([P, PACK, H], BF16, name=label)
            nc.sync.dma_start(
                out=raw[:].rearrange("p (u e) h -> p u e h", u=2),
                in_=w.rearrange("(u p e) h -> p u e h", u=2, e=2),
            )
            return raw

        load_unit(x, x_units, 0, "x_unit")
        load_unit(state, state_units, 0, "state_unit")
        w2_raw = load_weight(w2, "w2_raw")
        u2_raw = load_weight(u2, "u2_raw")
        load_unit(x, x_units, 1, "x_unit")
        load_unit(state, state_units, 1, "state_unit")
        for unit in range(2, N_UNITS + 2):
            if unit < N_UNITS:
                load_unit(x, x_units, unit, "x_unit")
                load_unit(state, state_units, unit, "state_unit")
            load_unit(c, c_units, unit - 2, "c_unit")

        def flip(loaded):
            words = loaded[:].bitcast(F32)
            flipped = psum.tile([P, 2, UNIT_ROWS], F32, name="flipped", tag="flipped", bufs=2)
            for tt in range(UNIT_TILES):
                for u in range(2):
                    nc.tensor.transpose(
                        flipped[:, u, tt * P : (tt + 1) * P],
                        words[:, tt, u * P : (u + 1) * P],
                        ident[:],
                    )
            return flipped

        def transpose_operands(unit):
            grouped = work.tile([P, 2, UNIT_ROWS, PACK], BF16, name="grouped", align_bytes=64)
            for operand, loaded in enumerate((x_units[unit], state_units[unit])):
                nc.scalar.copy(
                    out=grouped[:, operand, :, :].bitcast(F32),
                    in_=flip(loaded)[:].rearrange("p u r -> p r u"),
                )
            return grouped

        def quantise(grouped):
            codes = work.tile([P, 2 * UNIT_ROWS], U32, name="codes", align_bytes=64)
            scales = work.tile([P, 2 * UNIT_ROWS], U8, name="scales", align_bytes=64)
            nc.vector.quantize_mx(
                out=codes[:].bitcast(FP8X4),
                scales=scales[:],
                in_=grouped[:].rearrange("p o r t -> p (o r t)"),
            )
            return codes, scales

        def gate(codes, scales):
            x_cols = slice(0, UNIT_ROWS)
            state_cols = slice(UNIT_ROWS, 2 * UNIT_ROWS)
            gate_t = work.tile([P, H_TILES, UNIT_ROWS], F32, name="gate_t", bufs=4)
            for pair in range(H_TILES // 2):
                acc = psum.tile([P, 2, UNIT_ROWS], F32, name="acc", tag="acc")
                for half in range(2):
                    features = slice((2 * pair + half) * P, (2 * pair + half + 1) * P)
                    nc.tensor.matmul_mx(
                        out=acc[:, half, :],
                        lhsT=w2_codes[:, features].bitcast(FP8X4),
                        lhsT_scale=w2_scales[:, features],
                        rhs=codes[:, x_cols].bitcast(FP8X4),
                        rhs_scale=scales[:, x_cols],
                        start=True,
                        stop=False,
                    )
                    nc.tensor.matmul_mx(
                        out=acc[:, half, :],
                        lhsT=u2_codes[:, features].bitcast(FP8X4),
                        lhsT_scale=u2_scales[:, features],
                        rhs=codes[:, state_cols].bitcast(FP8X4),
                        rhs_scale=scales[:, state_cols],
                        start=False,
                        stop=True,
                    )
                for half in range(2):
                    m = 2 * pair + half
                    nc.scalar.activation(
                        out=gate_t[:, m, :],
                        in_=acc[:, half, :],
                        func=ACT.Sigmoid,
                        bias=bias_col[:, m : m + 1],
                        scale=1.0,
                    )
            return gate_t

        def corner_difference(unit):
            diff_t = psum.tile([P, P], F32, name="diff_t", tag="diff", bufs=1)
            for loaded, sign, first in ((state_units[unit], plus, True), (c_units[unit], minus, False)):
                nc.tensor.matmul(
                    diff_t[:], lhsT=loaded[:, 0, 0:P], rhs=sign[:], start=first, stop=not first
                )
            return diff_t

        def corner_product(gate_t, diff_t):
            product_t = work.tile([P, P], F32, name="product_t")
            nc.vector.tensor_tensor(
                out=product_t[:], in0=gate_t[:, 0, 0:P], in1=diff_t[:], op=ALU.mult
            )
            return product_t

        def subtract_and_store(unit, result, c_part, tiles, engine):
            cols = slice(tiles.start * H + (P if unit in products else 0), tiles.stop * H)
            flat = result[:].rearrange("p t h -> p (t h)")
            engine.tensor_tensor(
                out=flat[:, cols],
                in0=flat[:, cols],
                in1=c_part[:].rearrange("p t h -> p (t h)")[:, cols],
                op=ALU.subtract,
            )
            nc.sync.dma_start(out=rows_of(out, unit)[:, tiles, :], in_=result[:, tiles, :])

        def blend_and_store(unit, between):
            gate_t = gates[unit]
            result = work.tile([P, UNIT_TILES, H], F32, name="result", bufs=12)
            c_part = work.tile([P, UNIT_TILES, H], F32, name="c_part")
            for tt in range(UNIT_TILES):
                back = psum.tile([P, H], F32, name="back", tag="back", bufs=3)
                for m in range(H_TILES):
                    corner = tt == 0 and m == 0 and unit in products
                    nc.tensor.transpose(
                        back[:, m * P : (m + 1) * P],
                        products[unit][:] if corner else gate_t[:, m, tt * P : (tt + 1) * P],
                        ident[:],
                    )
                corner = tt == 0 and unit in products
                cols = slice(P if corner else 0, H)
                nc.vector.tensor_tensor(
                    out=result[:, tt, cols],
                    in0=back[:, cols],
                    in1=state_units[unit][:, tt, cols],
                    op=ALU.mult,
                )
                if corner:
                    nc.vector.tensor_tensor(
                        out=result[:, 0, 0:P],
                        in0=back[:, 0:P],
                        in1=c_units[unit][:, 0, 0:P],
                        op=ALU.add,
                    )
                if tt == UNIT_TILES - 1:
                    between()
                nc.vector.scalar_tensor_tensor(
                    out=c_part[:, tt, cols],
                    in0=back[:, cols],
                    scalar=1.0,
                    in1=c_units[unit][:, tt, cols],
                    op0=ALU.subtract,
                    op1=ALU.mult,
                )
                if unit >= N_UNITS - LAST_UNITS:
                    engine = nc.vector if unit == N_UNITS - 1 else nc.gpsimd
                    subtract_and_store(unit, result, c_part, slice(tt, tt + 1), engine)
            if unit < N_UNITS - LAST_UNITS:
                subtract_and_store(unit, result, c_part, slice(0, UNIT_TILES), nc.gpsimd)

        gates, products = {}, {}

        flipped_units = {0: transpose_operands(0)}
        bias_ps = psum.tile([P, H], F32, name="bias_ps", tag="back", bufs=3)
        nc.tensor.transpose(bias_ps[:, 0:P], bias_words[:], ident[:])
        bias_col = const.tile([P, H_TILES], F32, name="bias_col")
        nc.scalar.copy(out=bias_col[:], in_=bias_ps[:, 0:H_TILES])
        quantised = {0: quantise(flipped_units[0])}

        groups, operands = {}, {}
        for label in ("w2", "u2"):
            groups[label] = const.tile([P, H, PACK], BF16, name=label + "_grouped", align_bytes=64)
            codes = const.tile([P, H], U32, name=label + "_codes", align_bytes=64)
            scales = const.tile([P, H], U8, name=label + "_scales", align_bytes=64)
            operands[label] = (codes, scales)
        first, second = slice(0, HALF), slice(HALF, H)
        for label, raw, cols, copy in (
            ("w2", w2_raw, first, nc.vector.tensor_copy),
            ("u2", u2_raw, first, nc.scalar.copy),
            ("w2", w2_raw, second, nc.vector.tensor_copy),
            ("u2", u2_raw, second, nc.vector.tensor_copy),
        ):
            copy(out=groups[label][:, cols, :], in_=raw[:, :, cols].rearrange("p t h -> p h t"))
        for cols in (first, second):
            for label in ("w2", "u2"):
                codes, scales = operands[label]
                nc.vector.quantize_mx(
                    out=codes[:, cols].bitcast(FP8X4),
                    scales=scales[:, cols],
                    in_=groups[label][:, cols, :].rearrange("p h t -> p (h t)"),
                )
        w2_codes, w2_scales = operands["w2"]
        u2_codes, u2_scales = operands["u2"]

        for step in range(N_UNITS + BACK_LAG):
            if 0 < step < N_UNITS:
                quantised[step] = quantise(flipped_units[step])

            corner_unit = step - 1
            has_corner = 0 <= corner_unit < N_UNITS - LAST_UNITS
            if has_corner:
                diff_t = corner_difference(corner_unit)

            def corner_step():
                if has_corner:
                    products[corner_unit] = corner_product(gates[corner_unit], diff_t)

            if step >= BACK_LAG:
                blend_and_store(step - BACK_LAG, corner_step)
            else:
                corner_step()
            if step + FLIP_LEAD < N_UNITS:
                flipped_units[step + FLIP_LEAD] = transpose_operands(step + FLIP_LEAD)
            if step < N_UNITS:
                gates[step] = gate(*quantised[step])
